import numpy as np
import ml_dtypes


def mxq(x, axis, fmt="e4m3"):
    dtype, down = {"e4m3": (ml_dtypes.float8_e4m3fn, 7), "e5m2": (ml_dtypes.float8_e5m2, 14)}[fmt]
    v = np.moveaxis(np.asarray(x, np.float32).astype(ml_dtypes.bfloat16).astype(np.float64), axis, -1)
    blocks = v.reshape(v.shape[:-1] + (-1, 32))
    amax = np.abs(blocks).max(-1, keepdims=True)
    byte = np.maximum(np.where(amax > 0, np.frexp(amax)[1] - 1 + 127, 0) - down, 1)
    scale = np.exp2(byte - 127.0)
    codes = (blocks / scale).astype(np.float32).astype(dtype).astype(np.float64)
    return np.moveaxis((codes * scale).reshape(v.shape), -1, axis)


WIDE = False


def mx_kscale(k):
    if not WIDE:
        return np.ones(k)
    levels = np.array([20, -20, 10, -10, 0])
    a = np.random.permutation(np.resize(levels, k // 512 * 4)).reshape(k // 512, 4)
    idx = np.arange(k)
    return np.exp2(a[idx // 512, idx % 128 // 32])


BF16 = ml_dtypes.bfloat16


def bf(x):
    return np.asarray(x, np.float32).astype(BF16)


def f64(x):
    return np.asarray(x).astype(np.float64)


M, K, N = 8192, 512, 512


def setup_inputs():
    u = mx_kscale(N)
    A = np.tril(np.random.standard_normal((M, K)))
    B = np.tril(np.random.standard_normal((K, N))) * 1.5 / np.sqrt(K) / u
    g = np.random.standard_normal((M, N)) * np.exp2(np.random.randint(-12, 1, (M, 1))) * 8.0 * u
    return {"A": bf(A), "B": bf(B), "grad_out": bf(g)}


def reference(A, B, grad_out):
    g = np.tril(f64(grad_out))
    return mxq(g, 1, "e5m2") @ mxq(f64(B), 1, "e4m3").T

@@ -1,0 +1,143 @@
+from contextlib import ExitStack
+
+import concourse.mybir as mybir
+from concourse.masks import make_identity
+
+F32 = mybir.dt.float32
+BF16 = mybir.dt.bfloat16
+U32 = mybir.dt.uint32
+U8 = mybir.dt.uint8
+E4M3 = mybir.dt.float8_e4m3fn_x4
+E5M2 = mybir.dt.float8_e5m2_x4
+
+P = 128
+M, K, N = 8192, 512, 512
+HEAD = 512
+T_HEAD = HEAD // P
+T_MAIN = (M - HEAD) // P
+GROUP = 4
+CHUNKS = [4, 8, 16, 16, 16]
+STORE_GROUPS = 2
+LEAD = 2
+
+FLOPS = 2 * M * K * N
+BYTES = 2 * (M * N - HEAD * N + HEAD * (HEAD + 1) // 2) + 2 * (K * (K + 1) // 2) + 4 * M * K
+
+
+def tile_modelnew_t_kernel(tc, A, B, grad_out, out):
+    nc = tc.nc
+    assert sum(CHUNKS) == T_MAIN
+    with ExitStack() as ctx:
+        keep = ctx.enter_context(tc.tile_pool(name="keep", bufs=1))
+        work = ctx.enter_context(tc.tile_pool(name="work", bufs=3))
+        tpool = ctx.enter_context(tc.psum_pool(name="tpsum", bufs=4))
+        opool = ctx.enter_context(tc.psum_pool(name="opsum", bufs=4))
+
+        b_sb = keep.tile([P, GROUP * N], BF16, name="b_sb")
+        nc.sync.dma_start(
+            out=b_sb[:].rearrange("p (t n) -> p t n", t=GROUP),
+            in_=B.rearrange("(t p) n -> p t n", p=P),
+        )
+        g_main = grad_out[HEAD:M, :].rearrange("(p t) n -> p (t n)", t=T_MAIN)
+        o_main = out[HEAD:M, :].rearrange("(p t) k -> p (t k)", t=T_MAIN)
+        sources = []
+        first = 0
+        for c, size in enumerate(CHUNKS):
+            g_sb = keep.tile([P, size * N], BF16, name="g_sb%d" % c)
+            nc.sync.dma_start(out=g_sb[:], in_=g_main[:, first * N : (first + size) * N])
+            words = g_sb[:].bitcast(F32)
+            for s in range(size // GROUP):
+                sources.append(words[:, s * 1024 : (s + 1) * 1024])
+            first += size
+        h_sb = keep.tile([P, T_HEAD * N], BF16, name="h_sb")
+        nc.sync.dma_start(out=h_sb[:], in_=grad_out[0:HEAD, :].rearrange("(p t) n -> p (t n)", t=T_HEAD))
+        sources.append(h_sb[:].bitcast(F32))
+        n_groups = len(sources)
+        n_main = n_groups - 1
+
+        ident = keep.tile([P, P], F32, name="ident")
+        make_identity(nc, ident[:])
+
+        targets = []
+        stores = {}
+        for m0 in range(0, n_main, STORE_GROUPS):
+            cnt = min(STORE_GROUPS, n_main - m0)
+            o_sb = keep.tile([P, cnt * GROUP * K], F32, name="o_sb%d" % m0)
+            for s in range(cnt):
+                targets.append(o_sb[:, s * GROUP * K : (s + 1) * GROUP * K])
+            stores[m0 + cnt - 1] = (o_main[:, m0 * GROUP * K : (m0 + cnt) * GROUP * K], o_sb)
+        oh_sb = keep.tile([P, T_HEAD * K], F32, name="oh_sb")
+        targets.append(oh_sb[:])
+        stores[n_main] = (out[0:HEAD, :].rearrange("(p t) k -> p (t k)", t=T_HEAD), oh_sb)
+
+        def flip(words):
+            grouped = work.tile([P, GROUP * N], BF16, align_bytes=64)
+            g_words = grouped[:].bitcast(F32)
+            for h in range(2):
+                tp = tpool.tile([P, 512], F32)
+                for q in range(4):
+                    col = 512 * h + P * q
+                    nc.tensor.transpose(tp[:, P * q : P * (q + 1)], words[:, col : col + P], ident[:])
+                nc.vector.tensor_copy(
+                    out=g_words[:, 512 * h : 512 * (h + 1)].rearrange("p (i r u) -> p i r u", i=2, u=2),
+                    in_=tp[:].rearrange("p (i u r) -> p i r u", i=2, u=2),
+                )
+            return grouped
+
+        def quantise(pool, grouped, fmt):
+            codes = pool.tile([P, GROUP * P], U32, align_bytes=64)
+            scales = pool.tile([P, GROUP * P], U8, align_bytes=64)
+            nc.vector.quantize_mx(out=codes[:].bitcast(fmt), scales=scales[:], in_=grouped[:])
+            return codes, scales
+
+        b_codes, b_scales = quantise(keep, flip(b_sb[:].bitcast(F32)), E4M3)
+
+        def multiply(g, codes, scales):
+            for i in range(GROUP):
+                po = opool.tile([P, K], F32)
+                nc.tensor.matmul_mx(
+                    out=po[:],
+                    lhsT=codes[:, P * i : P * (i + 1)].bitcast(E5M2),
+                    lhsT_scale=scales[:, P * i : P * (i + 1)],
+                    rhs=b_codes[:].bitcast(E4M3),
+                    rhs_scale=b_scales[:],
+                    start=True,
+                    stop=True,
+                )
+                dst = targets[g][:, K * i : K * (i + 1)]
+                if i == GROUP - 1 and g % 2 == 1:
+                    nc.vector.tensor_copy(out=dst, in_=po[:])
+                else:
+                    nc.scalar.copy(out=dst, in_=po[:])
+            if g in stores:
+                dram, o_tile = stores[g]
+                nc.sync.dma_start(out=dram, in_=o_tile[:])
+
+        def mask_head_a():
+            h32 = keep.tile([P, T_HEAD * N], F32, name="h32")
+            nc.vector.tensor_copy(out=h32[:], in_=h_sb[:])
+            nc.gpsimd.affine_select(
+                out=h32[:],
+                in_=h32[:],
+                pattern=[[1, T_HEAD], [-1, N]],
+                compare_op=mybir.AluOpType.is_ge,
+                fill=0.0,
+                base=0,
+                channel_multiplier=T_HEAD,
+            )
+            return h32
+
+        grouped_of = {}
+        quantised_of = {}
+        h32 = None
+        for step in range(-LEAD, n_groups):
+            if step + LEAD == n_groups - 4:
+                h32 = mask_head_a()
+            if step + LEAD == n_groups - 2:
+                nc.vector.tensor_copy(out=h_sb[:], in_=h32[:])
+            if step + LEAD < n_groups:
+                grouped_of[step + LEAD] = flip(sources[step + LEAD])
+            if 0 <= step + LEAD - 1 < n_groups:
+                quantised_of[step + LEAD - 1] = quantise(work, grouped_of[step + LEAD - 1], E5M2)
+            if step >= 0:
+                multiply(step, quantised_of[step][0], quantised_of[step][1])

@@ -32,6 +32,7 @@ def tile_modelnew_t_kernel(tc, A, B, grad_out, out):
         work = ctx.enter_context(tc.tile_pool(name="work", bufs=3))
         tpool = ctx.enter_context(tc.psum_pool(name="tpsum", bufs=4))
         opool = ctx.enter_context(tc.psum_pool(name="opsum", bufs=4))
+        ctx.enter_context(tc.manual_schedule())
 
         b_sb = keep.tile([P, GROUP * N], BF16, name="b_sb")
         nc.sync.dma_start(

@@ -16,8 +16,9 @@ HEAD = 512
 T_HEAD = HEAD // P
 T_MAIN = (M - HEAD) // P
 GROUP = 4
-CHUNKS = [4, 8, 16, 16, 16]
-STORE_GROUPS = 2
+CHUNKS = [4, 8, 16, 32]
+STORES = [4, 4, 4, 2, 1]
+VECTOR_EVERY = 4
 LEAD = 2
 
 FLOPS = 2 * M * K * N
@@ -26,7 +27,7 @@ BYTES = 2 * (M * N - HEAD * N + HEAD * (HEAD + 1) // 2) + 2 * (K * (K + 1) // 2)
 
 def tile_modelnew_t_kernel(tc, A, B, grad_out, out):
     nc = tc.nc
-    assert sum(CHUNKS) == T_MAIN
+    assert sum(CHUNKS) == T_MAIN and sum(STORES) * GROUP == T_MAIN
     with ExitStack() as ctx:
         keep = ctx.enter_context(tc.tile_pool(name="keep", bufs=1))
         work = ctx.enter_context(tc.tile_pool(name="work", bufs=3))
@@ -34,11 +35,15 @@ def tile_modelnew_t_kernel(tc, A, B, grad_out, out):
         opool = ctx.enter_context(tc.psum_pool(name="opsum", bufs=4))
         ctx.enter_context(tc.manual_schedule())
 
+        def load_lower(dst, rows):
+            for r in range(GROUP):
+                live = P * (r + 1)
+                nc.sync.dma_start(out=dst[:, N * r : N * r + live], in_=rows[P * r : P * (r + 1), 0:live])
+                if live < N:
+                    nc.vector.memset(dst[:, N * r + live : N * (r + 1)], 0.0)
+
         b_sb = keep.tile([P, GROUP * N], BF16, name="b_sb")
-        nc.sync.dma_start(
-            out=b_sb[:].rearrange("p (t n) -> p t n", t=GROUP),
-            in_=B.rearrange("(t p) n -> p t n", p=P),
-        )
+        load_lower(b_sb, B)
         g_main = grad_out[HEAD:M, :].rearrange("(p t) n -> p (t n)", t=T_MAIN)
         o_main = out[HEAD:M, :].rearrange("(p t) k -> p (t k)", t=T_MAIN)
         sources = []
@@ -50,9 +55,9 @@ def tile_modelnew_t_kernel(tc, A, B, grad_out, out):
             for s in range(size // GROUP):
                 sources.append(words[:, s * 1024 : (s + 1) * 1024])
             first += size
-        h_sb = keep.tile([P, T_HEAD * N], BF16, name="h_sb")
-        nc.sync.dma_start(out=h_sb[:], in_=grad_out[0:HEAD, :].rearrange("(p t) n -> p (t n)", t=T_HEAD))
-        sources.append(h_sb[:].bitcast(F32))
+        h_sb = keep.tile([P, T_HEAD * (N + P)], BF16, name="h_sb")
+        load_lower(h_sb, grad_out)
+        sources.append(h_sb[:, 0 : T_HEAD * N].bitcast(F32))
         n_groups = len(sources)
         n_main = n_groups - 1
 
@@ -61,15 +66,19 @@ def tile_modelnew_t_kernel(tc, A, B, grad_out, out):
 
         targets = []
         stores = {}
-        for m0 in range(0, n_main, STORE_GROUPS):
-            cnt = min(STORE_GROUPS, n_main - m0)
+        m0 = 0
+        for cnt in STORES:
             o_sb = keep.tile([P, cnt * GROUP * K], F32, name="o_sb%d" % m0)
             for s in range(cnt):
                 targets.append(o_sb[:, s * GROUP * K : (s + 1) * GROUP * K])
-            stores[m0 + cnt - 1] = (o_main[:, m0 * GROUP * K : (m0 + cnt) * GROUP * K], o_sb)
+            stores[m0 + cnt - 1] = (o_main[:, m0 * GROUP * K : (m0 + cnt) * GROUP * K], o_sb[:])
+            m0 += cnt
         oh_sb = keep.tile([P, T_HEAD * K], F32, name="oh_sb")
         targets.append(oh_sb[:])
-        stores[n_main] = (out[0:HEAD, :].rearrange("(p t) k -> p (t k)", t=T_HEAD), oh_sb)
+        stores[n_main] = (
+            out[0:HEAD, :].rearrange("(t p) k -> p t k", p=P),
+            oh_sb[:].rearrange("p (t k) -> p t k", t=T_HEAD),
+        )
 
         def flip(words):
             grouped = work.tile([P, GROUP * N], BF16, align_bytes=64)
@@ -106,36 +115,33 @@ def tile_modelnew_t_kernel(tc, A, B, grad_out, out):
                     stop=True,
                 )
                 dst = targets[g][:, K * i : K * (i + 1)]
-                if i == GROUP - 1 and g % 2 == 1:
+                if i == GROUP - 1 and g % VECTOR_EVERY == VECTOR_EVERY - 1:
                     nc.vector.tensor_copy(out=dst, in_=po[:])
                 else:
                     nc.scalar.copy(out=dst, in_=po[:])
             if g in stores:
-                dram, o_tile = stores[g]
-                nc.sync.dma_start(out=dram, in_=o_tile[:])
+                nc.sync.dma_start(out=stores[g][0], in_=stores[g][1])
 
-        def mask_head_a():
-            h32 = keep.tile([P, T_HEAD * N], F32, name="h32")
-            nc.vector.tensor_copy(out=h32[:], in_=h_sb[:])
-            nc.gpsimd.affine_select(
-                out=h32[:],
-                in_=h32[:],
-                pattern=[[1, T_HEAD], [-1, N]],
-                compare_op=mybir.AluOpType.is_ge,
-                fill=0.0,
-                base=0,
-                channel_multiplier=T_HEAD,
-            )
-            return h32
+        diag = h_sb[:].rearrange("p (r c) -> p r c", c=N + P)[:, :, 0:P]
+        d32 = keep.tile([P, T_HEAD * P], F32, name="d32")
+        d32_blocks = d32[:].rearrange("p (r c) -> p r c", c=P)
 
         grouped_of = {}
         quantised_of = {}
-        h32 = None
         for step in range(-LEAD, n_groups):
             if step + LEAD == n_groups - 4:
-                h32 = mask_head_a()
+                nc.vector.tensor_copy(out=d32_blocks, in_=diag)
+                nc.gpsimd.affine_select(
+                    out=d32[:],
+                    in_=d32[:],
+                    pattern=[[0, T_HEAD], [-1, P]],
+                    compare_op=mybir.AluOpType.is_ge,
+                    fill=0.0,
+                    base=0,
+                    channel_multiplier=1,
+                )
             if step + LEAD == n_groups - 2:
-                nc.vector.tensor_copy(out=h_sb[:], in_=h32[:])
+                nc.vector.tensor_copy(out=diag, in_=d32_blocks)
             if step + LEAD < n_groups:
                 grouped_of[step + LEAD] = flip(sources[step + LEAD])
             if 0 <= step + LEAD - 1 < n_groups:

@@ -16,8 +16,8 @@ HEAD = 512
 T_HEAD = HEAD // P
 T_MAIN = (M - HEAD) // P
 GROUP = 4
-CHUNKS = [4, 8, 16, 32]
-STORES = [4, 4, 4, 2, 1]
+CHUNKS = [4, 8, 16, 16, 16]
+STORES = [2, 2, 2, 2, 2, 2, 2, 1]
 VECTOR_EVERY = 4
 LEAD = 2
 

@@ -20,6 +20,7 @@ CHUNKS = [4, 8, 16, 16, 16]
 STORES = [2, 2, 2, 2, 2, 2, 2, 1]
 VECTOR_EVERY = 4
 LEAD = 2
+DMA_ALIGN = 256
 
 FLOPS = 2 * M * K * N
 BYTES = 2 * (M * N - HEAD * N + HEAD * (HEAD + 1) // 2) + 2 * (K * (K + 1) // 2) + 4 * M * K
@@ -42,20 +43,20 @@ def tile_modelnew_t_kernel(tc, A, B, grad_out, out):
                 if live < N:
                     nc.vector.memset(dst[:, N * r + live : N * (r + 1)], 0.0)
 
-        b_sb = keep.tile([P, GROUP * N], BF16, name="b_sb")
+        b_sb = keep.tile([P, GROUP * N], BF16, name="b_sb", align_bytes=DMA_ALIGN)
         load_lower(b_sb, B)
         g_main = grad_out[HEAD:M, :].rearrange("(p t) n -> p (t n)", t=T_MAIN)
         o_main = out[HEAD:M, :].rearrange("(p t) k -> p (t k)", t=T_MAIN)
         sources = []
         first = 0
         for c, size in enumerate(CHUNKS):
-            g_sb = keep.tile([P, size * N], BF16, name="g_sb%d" % c)
+            g_sb = keep.tile([P, size * N], BF16, name="g_sb%d" % c, align_bytes=DMA_ALIGN)
             nc.sync.dma_start(out=g_sb[:], in_=g_main[:, first * N : (first + size) * N])
             words = g_sb[:].bitcast(F32)
             for s in range(size // GROUP):
                 sources.append(words[:, s * 1024 : (s + 1) * 1024])
             first += size
-        h_sb = keep.tile([P, T_HEAD * (N + P)], BF16, name="h_sb")
+        h_sb = keep.tile([P, T_HEAD * (N + P)], BF16, name="h_sb", align_bytes=DMA_ALIGN)
         load_lower(h_sb, grad_out)
         sources.append(h_sb[:, 0 : T_HEAD * N].bitcast(F32))
         n_groups = len(sources)
@@ -68,12 +69,12 @@ def tile_modelnew_t_kernel(tc, A, B, grad_out, out):
         stores = {}
         m0 = 0
         for cnt in STORES:
-            o_sb = keep.tile([P, cnt * GROUP * K], F32, name="o_sb%d" % m0)
+            o_sb = keep.tile([P, cnt * GROUP * K], F32, name="o_sb%d" % m0, align_bytes=DMA_ALIGN)
             for s in range(cnt):
                 targets.append(o_sb[:, s * GROUP * K : (s + 1) * GROUP * K])
             stores[m0 + cnt - 1] = (o_main[:, m0 * GROUP * K : (m0 + cnt) * GROUP * K], o_sb[:])
             m0 += cnt
-        oh_sb = keep.tile([P, T_HEAD * K], F32, name="oh_sb")
+        oh_sb = keep.tile([P, T_HEAD * K], F32, name="oh_sb", align_bytes=DMA_ALIGN)
         targets.append(oh_sb[:])
         stores[n_main] = (
             out[0:HEAD, :].rearrange("(t p) k -> p t k", p=P),

@@ -17,7 +17,7 @@ T_HEAD = HEAD // P
 T_MAIN = (M - HEAD) // P
 GROUP = 4
 CHUNKS = [4, 8, 16, 16, 16]
-STORES = [2, 2, 2, 2, 2, 2, 2, 1]
+STORE_GROUPS = 2
 VECTOR_EVERY = 4
 LEAD = 2
 DMA_ALIGN = 256
@@ -28,7 +28,7 @@ BYTES = 2 * (M * N - HEAD * N + HEAD * (HEAD + 1) // 2) + 2 * (K * (K + 1) // 2)
 
 def tile_modelnew_t_kernel(tc, A, B, grad_out, out):
     nc = tc.nc
-    assert sum(CHUNKS) == T_MAIN and sum(STORES) * GROUP == T_MAIN
+    assert sum(CHUNKS) == T_MAIN
     with ExitStack() as ctx:
         keep = ctx.enter_context(tc.tile_pool(name="keep", bufs=1))
         work = ctx.enter_context(tc.tile_pool(name="work", bufs=3))
@@ -45,13 +45,16 @@ def tile_modelnew_t_kernel(tc, A, B, grad_out, out):
 
         b_sb = keep.tile([P, GROUP * N], BF16, name="b_sb", align_bytes=DMA_ALIGN)
         load_lower(b_sb, B)
-        g_main = grad_out[HEAD:M, :].rearrange("(p t) n -> p (t n)", t=T_MAIN)
-        o_main = out[HEAD:M, :].rearrange("(p t) k -> p (t k)", t=T_MAIN)
         sources = []
+        o_views = []
         first = 0
         for c, size in enumerate(CHUNKS):
+            row0 = HEAD + P * first
             g_sb = keep.tile([P, size * N], BF16, name="g_sb%d" % c, align_bytes=DMA_ALIGN)
-            nc.sync.dma_start(out=g_sb[:], in_=g_main[:, first * N : (first + size) * N])
+            nc.sync.dma_start(
+                out=g_sb[:], in_=grad_out[row0 : row0 + P * size, :].rearrange("(p t) n -> p (t n)", t=size)
+            )
+            o_views.append(out[row0 : row0 + P * size, :].rearrange("(p t) k -> p (t k)", t=size))
             words = g_sb[:].bitcast(F32)
             for s in range(size // GROUP):
                 sources.append(words[:, s * 1024 : (s + 1) * 1024])
@@ -68,12 +71,14 @@ def tile_modelnew_t_kernel(tc, A, B, grad_out, out):
         targets = []
         stores = {}
         m0 = 0
-        for cnt in STORES:
-            o_sb = keep.tile([P, cnt * GROUP * K], F32, name="o_sb%d" % m0, align_bytes=DMA_ALIGN)
-            for s in range(cnt):
-                targets.append(o_sb[:, s * GROUP * K : (s + 1) * GROUP * K])
-            stores[m0 + cnt - 1] = (o_main[:, m0 * GROUP * K : (m0 + cnt) * GROUP * K], o_sb[:])
-            m0 += cnt
+        for c, size in enumerate(CHUNKS):
+            for s0 in range(0, size // GROUP, STORE_GROUPS):
+                cnt = min(STORE_GROUPS, size // GROUP - s0)
+                o_sb = keep.tile([P, cnt * GROUP * K], F32, name="o_sb%d" % m0, align_bytes=DMA_ALIGN)
+                for s in range(cnt):
+                    targets.append(o_sb[:, s * GROUP * K : (s + 1) * GROUP * K])
+                stores[m0 + cnt - 1] = (o_views[c][:, s0 * GROUP * K : (s0 + cnt) * GROUP * K], o_sb[:])
+                m0 += cnt
         oh_sb = keep.tile([P, T_HEAD * K], F32, name="oh_sb", align_bytes=DMA_ALIGN)
         targets.append(oh_sb[:])
         stores[n_main] = (

from contextlib import ExitStack

import concourse.mybir as mybir
from concourse.masks import make_identity

F32 = mybir.dt.float32
BF16 = mybir.dt.bfloat16
U32 = mybir.dt.uint32
U8 = mybir.dt.uint8
E4M3 = mybir.dt.float8_e4m3fn_x4
E5M2 = mybir.dt.float8_e5m2_x4

P = 128
M, K, N = 8192, 512, 512
HEAD = 512
T_HEAD = HEAD // P
T_MAIN = (M - HEAD) // P
GROUP = 4
CHUNKS = [4, 8, 16, 16, 16]
STORE_GROUPS = 2
VECTOR_EVERY = 4
LEAD = 2
DMA_ALIGN = 256

FLOPS = 2 * M * K * N
BYTES = 2 * (M * N - HEAD * N + HEAD * (HEAD + 1) // 2) + 2 * (K * (K + 1) // 2) + 4 * M * K


def tile_modelnew_t_kernel(tc, A, B, grad_out, out):
    nc = tc.nc
    assert sum(CHUNKS) == T_MAIN
    with ExitStack() as ctx:
        keep = ctx.enter_context(tc.tile_pool(name="keep", bufs=1))
        work = ctx.enter_context(tc.tile_pool(name="work", bufs=3))
        tpool = ctx.enter_context(tc.psum_pool(name="tpsum", bufs=4))
        opool = ctx.enter_context(tc.psum_pool(name="opsum", bufs=4))
        ctx.enter_context(tc.manual_schedule())

        def load_lower(dst, rows):
            for r in range(GROUP):
                live = P * (r + 1)
                nc.sync.dma_start(out=dst[:, N * r : N * r + live], in_=rows[P * r : P * (r + 1), 0:live])
                if live < N:
                    nc.vector.memset(dst[:, N * r + live : N * (r + 1)], 0.0)

        b_sb = keep.tile([P, GROUP * N], BF16, name="b_sb", align_bytes=DMA_ALIGN)
        load_lower(b_sb, B)
        sources = []
        o_views = []
        first = 0
        for c, size in enumerate(CHUNKS):
            row0 = HEAD + P * first
            g_sb = keep.tile([P, size * N], BF16, name="g_sb%d" % c, align_bytes=DMA_ALIGN)
            nc.sync.dma_start(
                out=g_sb[:], in_=grad_out[row0 : row0 + P * size, :].rearrange("(p t) n -> p (t n)", t=size)
            )
            o_views.append(out[row0 : row0 + P * size, :].rearrange("(p t) k -> p (t k)", t=size))
            words = g_sb[:].bitcast(F32)
            for s in range(size // GROUP):
                sources.append(words[:, s * 1024 : (s + 1) * 1024])
            first += size
        h_sb = keep.tile([P, T_HEAD * (N + P)], BF16, name="h_sb", align_bytes=DMA_ALIGN)
        load_lower(h_sb, grad_out)
        sources.append(h_sb[:, 0 : T_HEAD * N].bitcast(F32))
        n_groups = len(sources)
        n_main = n_groups - 1

        ident = keep.tile([P, P], F32, name="ident")
        make_identity(nc, ident[:])

        targets = []
        stores = {}
        m0 = 0
        for c, size in enumerate(CHUNKS):
            for s0 in range(0, size // GROUP, STORE_GROUPS):
                cnt = min(STORE_GROUPS, size // GROUP - s0)
                o_sb = keep.tile([P, cnt * GROUP * K], F32, name="o_sb%d" % m0, align_bytes=DMA_ALIGN)
                for s in range(cnt):
                    targets.append(o_sb[:, s * GROUP * K : (s + 1) * GROUP * K])
                stores[m0 + cnt - 1] = (o_views[c][:, s0 * GROUP * K : (s0 + cnt) * GROUP * K], o_sb[:])
                m0 += cnt
        oh_sb = keep.tile([P, T_HEAD * K], F32, name="oh_sb", align_bytes=DMA_ALIGN)
        targets.append(oh_sb[:])
        stores[n_main] = (
            out[0:HEAD, :].rearrange("(t p) k -> p t k", p=P),
            oh_sb[:].rearrange("p (t k) -> p t k", t=T_HEAD),
        )

        def flip(words):
            grouped = work.tile([P, GROUP * N], BF16, align_bytes=64)
            g_words = grouped[:].bitcast(F32)
            for h in range(2):
                tp = tpool.tile([P, 512], F32)
                for q in range(4):
                    col = 512 * h + P * q
                    nc.tensor.transpose(tp[:, P * q : P * (q + 1)], words[:, col : col + P], ident[:])
                nc.vector.tensor_copy(
                    out=g_words[:, 512 * h : 512 * (h + 1)].rearrange("p (i r u) -> p i r u", i=2, u=2),
                    in_=tp[:].rearrange("p (i u r) -> p i r u", i=2, u=2),
                )
            return grouped

        def quantise(pool, grouped, fmt):
            codes = pool.tile([P, GROUP * P], U32, align_bytes=64)
            scales = pool.tile([P, GROUP * P], U8, align_bytes=64)
            nc.vector.quantize_mx(out=codes[:].bitcast(fmt), scales=scales[:], in_=grouped[:])
            return codes, scales

        b_codes, b_scales = quantise(keep, flip(b_sb[:].bitcast(F32)), E4M3)

        def multiply(g, codes, scales):
            for i in range(GROUP):
                po = opool.tile([P, K], F32)
                nc.tensor.matmul_mx(
                    out=po[:],
                    lhsT=codes[:, P * i : P * (i + 1)].bitcast(E5M2),
                    lhsT_scale=scales[:, P * i : P * (i + 1)],
                    rhs=b_codes[:].bitcast(E4M3),
                    rhs_scale=b_scales[:],
                    start=True,
                    stop=True,
                )
                dst = targets[g][:, K * i : K * (i + 1)]
                if i == GROUP - 1 and g % VECTOR_EVERY == VECTOR_EVERY - 1:
                    nc.vector.tensor_copy(out=dst, in_=po[:])
                else:
                    nc.scalar.copy(out=dst, in_=po[:])
            if g in stores:
                nc.sync.dma_start(out=stores[g][0], in_=stores[g][1])

        diag = h_sb[:].rearrange("p (r c) -> p r c", c=N + P)[:, :, 0:P]
        d32 = keep.tile([P, T_HEAD * P], F32, name="d32")
        d32_blocks = d32[:].rearrange("p (r c) -> p r c", c=P)

        grouped_of = {}
        quantised_of = {}
        for step in range(-LEAD, n_groups):
            if step + LEAD == n_groups - 4:
                nc.vector.tensor_copy(out=d32_blocks, in_=diag)
                nc.gpsimd.affine_select(
                    out=d32[:],
                    in_=d32[:],
                    pattern=[[0, T_HEAD], [-1, P]],
                    compare_op=mybir.AluOpType.is_ge,
                    fill=0.0,
                    base=0,
                    channel_multiplier=1,
                )
            if step + LEAD == n_groups - 2:
                nc.vector.tensor_copy(out=diag, in_=d32_blocks)
            if step + LEAD < n_groups:
                grouped_of[step + LEAD] = flip(sources[step + LEAD])
            if 0 <= step + LEAD - 1 < n_groups:
                quantised_of[step + LEAD - 1] = quantise(work, grouped_of[step + LEAD - 1], E5M2)
            if step >= 0:
                multiply(step, quantised_of[step][0], quantised_of[step][1])
